import numpy as np
import ml_dtypes


def mxq(x, axis, fmt="e4m3"):
    dtype, down = {"e4m3": (ml_dtypes.float8_e4m3fn, 7), "e5m2": (ml_dtypes.float8_e5m2, 14)}[fmt]
    v = np.moveaxis(np.asarray(x, np.float32).astype(ml_dtypes.bfloat16).astype(np.float64), axis, -1)
    blocks = v.reshape(v.shape[:-1] + (-1, 32))
    amax = np.abs(blocks).max(-1, keepdims=True)
    byte = np.maximum(np.where(amax > 0, np.frexp(amax)[1] - 1 + 127, 0) - down, 1)
    scale = np.exp2(byte - 127.0)
    codes = (blocks / scale).astype(np.float32).astype(dtype).astype(np.float64)
    return np.moveaxis((codes * scale).reshape(v.shape), -1, axis)


WIDE = False


def mx_kscale(k):
    if not WIDE:
        return np.ones(k)
    levels = np.array([10, -10, 5, -5, 0])
    a = np.random.permutation(np.resize(levels, k // 512 * 4)).reshape(k // 512, 4)
    idx = np.arange(k)
    return np.exp2(a[idx // 512, idx % 128 // 32])


BF16 = ml_dtypes.bfloat16


def bf(x):
    return np.asarray(x, np.float32).astype(BF16)


def f64(x):
    return np.asarray(x).astype(np.float64)


N, C = 4096, 256
KV = 2 * C
SQRT2 = np.sqrt(2.0)
EPS = 1e-6


def setup_inputs():
    t = mx_kscale(KV)
    return {"s": bf(np.random.standard_normal((N, C))),
            "v": bf(np.random.standard_normal((N, C, 3))),
            "g_v": bf(np.random.standard_normal((N, KV)) * t),
            "wv": bf(np.random.standard_normal((KV, C)) / t[:, None]),
            "ln_g1": bf(1.0 + 0.1 * np.random.standard_normal(C))}


def reference(s, v, g_v, wv, ln_g1):
    s, v = f64(s), f64(v)
    sv = SQRT2 * s[..., None] * v
    vec = np.concatenate([v, sv], axis=1) * f64(g_v)[..., None]
    dv = (mxq(vec.transpose(0, 2, 1), 2, "e4m3") @ mxq(f64(wv), 0, "e4m3")) / np.sqrt(KV)
    y = v + dv.transpose(0, 2, 1)
    rms = np.sqrt(np.mean(y * y, axis=(1, 2), keepdims=True) + EPS)
    return y / rms * f64(ln_g1)[None, :, None]

@@ -1,0 +1,170 @@
+import math
+from contextlib import ExitStack
+
+import concourse.mybir as mybir
+from concourse.masks import make_identity
+
+BF16 = mybir.dt.bfloat16
+F32 = mybir.dt.float32
+U32 = mybir.dt.uint32
+U8 = mybir.dt.uint8
+FP8X4 = mybir.dt.float8_e4m3fn_x4
+MULT = mybir.AluOpType.mult
+ADD = mybir.AluOpType.add
+ACT = mybir.ActivationFunctionType
+
+P = 128
+POINTS = 4096
+C = 256
+DIMS = 3
+KV = 2 * C
+PACK = 4
+TILES = POINTS // P
+GROUP = 4
+GROUPS = TILES // GROUP
+HALVES = C // P
+EPS = 1e-6
+
+FLOPS = 2 * POINTS * DIMS * KV * C
+
+
+def tile_selfinteraction_pb_t_kernel(tc, s, v, g_v, wv, ln_g1, out):
+    nc = tc.nc
+    with ExitStack() as ctx:
+        const = ctx.enter_context(tc.tile_pool(name="const", bufs=1))
+        gate_pool = ctx.enter_context(tc.tile_pool(name="gate_pool", bufs=3))
+        mx_pool = ctx.enter_context(tc.tile_pool(name="mx_pool", bufs=2))
+        y_pool = ctx.enter_context(tc.tile_pool(name="y_pool", bufs=4))
+        o_pool = ctx.enter_context(tc.tile_pool(name="o_pool", bufs=2 * GROUP))
+        stat_pool = ctx.enter_context(tc.tile_pool(name="stat_pool", bufs=2))
+        flip_psum = ctx.enter_context(tc.psum_pool(name="flip_psum", bufs=2))
+        dv_psum = ctx.enter_context(tc.psum_pool(name="dv_psum", bufs=4))
+
+        s_dram = s.rearrange("(p i) c -> p i c", i=TILES)
+        g_dram = g_v.rearrange("(p i) m -> p i m", i=TILES)
+        v_dram = v.rearrange("(p i) c d -> p i c d", i=TILES)
+        out_dram = out.rearrange("(p i) c d -> p i c d", i=TILES)
+
+        wv_rows = const.tile([P, PACK, C], BF16)
+        nc.sync.dma_start(out=wv_rows[:], in_=wv.rearrange("(t p) c -> p t c", p=P))
+        s_sb = const.tile([P, TILES, C], BF16)
+        g_sb = const.tile([P, TILES, KV], BF16)
+        v_sb = const.tile([P, TILES, C, DIMS], BF16)
+        gain_sb = const.tile([P, C], BF16)
+        for g in range(GROUPS):
+            rows = slice(g * GROUP, (g + 1) * GROUP)
+            nc.sync.dma_start(out=s_sb[:, rows, :], in_=s_dram[:, rows, :])
+            nc.sync.dma_start(out=g_sb[:, rows, :], in_=g_dram[:, rows, :])
+            nc.sync.dma_start(out=v_sb[:, rows, :, :], in_=v_dram[:, rows, :, :])
+            if g == 0:
+                nc.sync.dma_start(out=gain_sb[:], in_=ln_g1.partition_broadcast(P))
+
+        ident_bf16 = const.tile([P, P], BF16)
+        make_identity(nc, ident_bf16[:])
+        ident_f32 = const.tile([P, P], F32)
+        make_identity(nc, ident_f32[:])
+        eps_sb = const.tile([P, 1], F32)
+        nc.vector.memset(eps_sb[:], EPS)
+
+        wv_grouped = const.tile([P, C, PACK], BF16, align_bytes=64)
+        nc.vector.tensor_copy(out=wv_grouped[:], in_=wv_rows[:].rearrange("p t c -> p c t"))
+        wv_codes = const.tile([P, C], U32, align_bytes=64)
+        wv_scales = const.tile([P, C], U8, align_bytes=64)
+        nc.vector.quantize_mx(
+            out=wv_codes[:].bitcast(FP8X4),
+            scales=wv_scales[:],
+            in_=wv_grouped[:].rearrange("p c t -> p (c t)"),
+        )
+
+        def gated_tile(i, u_grouped, k):
+            sg = gate_pool.tile([P, C], F32, tag="sg")
+            nc.gpsimd.tensor_tensor(out=sg[:], in0=s_sb[:, i, :], in1=g_sb[:, i, C:KV], op=MULT)
+            vg_t = flip_psum.tile([P, 2 * DIMS + 2, P], BF16, tag="vg_t")
+            for j in range(HALVES):
+                cols = slice(j * P, (j + 1) * P)
+                for d in range(DIMS):
+                    nc.tensor.transpose(
+                        out=vg_t[:, DIMS * j + d, :], in_=v_sb[:, i, cols, d], identity=ident_bf16[:]
+                    )
+                nc.tensor.transpose(
+                    out=vg_t[:, 2 * DIMS + j, :], in_=g_sb[:, i, cols], identity=ident_bf16[:]
+                )
+            sg_t = flip_psum.tile([P, HALVES, P], F32, tag="sg_t")
+            for j in range(HALVES):
+                cols = slice(j * P, (j + 1) * P)
+                nc.tensor.transpose(out=sg_t[:, j, :], in_=sg[:, cols], identity=ident_f32[:])
+            gates = gate_pool.tile([P, PACK, P], F32, tag="gates")
+            nc.scalar.copy(out=gates[:, 0:HALVES, :], in_=vg_t[:, 2 * DIMS : 2 * DIMS + HALVES, :])
+            nc.scalar.mul(out=gates[:, HALVES:PACK, :], in_=sg_t[:], mul=math.sqrt(2.0))
+            shape = [P, DIMS, P, 2, HALVES]
+            nc.vector.tensor_tensor(
+                out=u_grouped[:, :, k, :, :].rearrange("p d n (h j) -> p d n h j", j=HALVES),
+                in0=vg_t[:, 0 : 2 * DIMS, :]
+                .rearrange("p (j d) n -> p d n j", d=DIMS)
+                .unsqueeze(3)
+                .to_broadcast(shape),
+                in1=gates[:].rearrange("p (h j) n -> p n h j", j=HALVES).unsqueeze(1).to_broadcast(shape),
+                op=MULT,
+            )
+
+        for g in range(GROUPS):
+            u_grouped = mx_pool.tile([P, DIMS, GROUP, P, PACK], BF16, align_bytes=64, tag="u_grouped")
+            for k in range(GROUP):
+                gated_tile(g * GROUP + k, u_grouped, k)
+
+            u_codes = mx_pool.tile([P, DIMS, GROUP * P], U32, align_bytes=64, tag="u_codes")
+            u_scales = mx_pool.tile([P, DIMS, GROUP * P], U8, align_bytes=64, tag="u_scales")
+            for d in range(DIMS):
+                nc.vector.quantize_mx(
+                    out=u_codes[:, d, :].bitcast(FP8X4),
+                    scales=u_scales[:, d, :],
+                    in_=u_grouped[:, d, :, :, :].rearrange("p k n t -> p (k n t)"),
+                )
+
+            sum_sq = stat_pool.tile([P, GROUP], F32, tag="sum_sq")
+            scaled = []
+            for k in range(GROUP):
+                i = g * GROUP + k
+                points = slice(k * P, (k + 1) * P)
+                y = y_pool.tile([P, C, DIMS], F32, tag="y")
+                for half in range(HALVES):
+                    cols = slice(half * P, (half + 1) * P)
+                    dv = dv_psum.tile([P, DIMS, P], F32, tag="dv")
+                    for d in range(DIMS):
+                        nc.tensor.matmul_mx(
+                            out=dv[:, d, :],
+                            lhsT=u_codes[:, d, points].bitcast(FP8X4),
+                            lhsT_scale=u_scales[:, d, points],
+                            rhs=wv_codes[:, cols].bitcast(FP8X4),
+                            rhs_scale=wv_scales[:, cols],
+                            start=True,
+                            stop=True,
+                        )
+                    nc.vector.scalar_tensor_tensor(
+                        out=y[:, cols, :],
+                        in0=dv[:].rearrange("p d c -> p c d"),
+                        scalar=1.0 / math.sqrt(KV),
+                        in1=v_sb[:, i, cols, :],
+                        op0=MULT,
+                        op1=ADD,
+                    )
+                squares = y_pool.tile([P, C, DIMS], BF16, tag="squares")
+                nc.scalar.activation(
+                    out=squares[:], in_=y[:], func=ACT.Square, accum_out=sum_sq[:, k : k + 1]
+                )
+                o = o_pool.tile([P, C, DIMS], F32, tag="o")
+                nc.gpsimd.tensor_tensor(
+                    out=o[:], in0=y[:], in1=gain_sb[:].unsqueeze(2).to_broadcast([P, C, DIMS]), op=MULT
+                )
+                scaled.append(o)
+
+            rms = stat_pool.tile([P, GROUP], F32, tag="rms")
+            nc.scalar.activation(
+                out=rms[:], in_=sum_sq[:], func=ACT.Sqrt, bias=eps_sb[:], scale=1.0 / (C * DIMS)
+            )
+            inv_rms = stat_pool.tile([P, GROUP], F32, tag="inv_rms")
+            nc.vector.reciprocal(out=inv_rms[:], in_=rms[:])
+            for k in range(GROUP):
+                o = scaled[k]
+                nc.scalar.activation(out=o[:], in_=o[:], func=ACT.Copy, scale=inv_rms[:, k : k + 1])
+                nc.sync.dma_start(out=out_dram[:, g * GROUP + k, :, :], in_=o[:])

@@ -93,19 +93,22 @@ def tile_selfinteraction_pb_t_kernel(tc, s, v, g_v, wv, ln_g1, out):
             for j in range(HALVES):
                 cols = slice(j * P, (j + 1) * P)
                 nc.tensor.transpose(out=sg_t[:, j, :], in_=sg[:, cols], identity=ident_f32[:])
-            gates = gate_pool.tile([P, PACK, P], F32, tag="gates")
-            nc.scalar.copy(out=gates[:, 0:HALVES, :], in_=vg_t[:, 2 * DIMS : 2 * DIMS + HALVES, :])
-            nc.scalar.mul(out=gates[:, HALVES:PACK, :], in_=sg_t[:], mul=math.sqrt(2.0))
-            shape = [P, DIMS, P, 2, HALVES]
-            nc.vector.tensor_tensor(
-                out=u_grouped[:, :, k, :, :].rearrange("p d n (h j) -> p d n h j", j=HALVES),
-                in0=vg_t[:, 0 : 2 * DIMS, :]
-                .rearrange("p (j d) n -> p d n j", d=DIMS)
-                .unsqueeze(3)
-                .to_broadcast(shape),
-                in1=gates[:].rearrange("p (h j) n -> p n h j", j=HALVES).unsqueeze(1).to_broadcast(shape),
-                op=MULT,
+            gates = gate_pool.tile([P, 2, P, HALVES], F32, tag="gates")
+            nc.scalar.copy(
+                out=gates[:, 0, :, :],
+                in_=vg_t[:, 2 * DIMS : 2 * DIMS + HALVES, :].rearrange("p j n -> p n j"),
             )
+            nc.scalar.mul(
+                out=gates[:, 1, :, :], in_=sg_t[:].rearrange("p j n -> p n j"), mul=math.sqrt(2.0)
+            )
+            v_t = vg_t[:, 0 : 2 * DIMS, :].rearrange("p (j d) n -> p d n j", d=DIMS)
+            for d in range(DIMS):
+                nc.vector.tensor_tensor(
+                    out=u_grouped[:, d, k, :, :].rearrange("p n (h j) -> p n h j", j=HALVES),
+                    in0=v_t[:, d, :, :].unsqueeze(2).to_broadcast([P, P, 2, HALVES]),
+                    in1=gates[:].rearrange("p h n j -> p n h j"),
+                    op=MULT,
+                )
 
         for g in range(GROUPS):
             u_grouped = mx_pool.tile([P, DIMS, GROUP, P, PACK], BF16, align_bytes=64, tag="u_grouped")

@@ -20,7 +20,7 @@ DIMS = 3
 KV = 2 * C
 PACK = 4
 TILES = POINTS // P
-GROUP = 4
+GROUP = 2
 GROUPS = TILES // GROUP
 HALVES = C // P
 EPS = 1e-6
@@ -32,13 +32,15 @@ def tile_selfinteraction_pb_t_kernel(tc, s, v, g_v, wv, ln_g1, out):
     nc = tc.nc
     with ExitStack() as ctx:
         const = ctx.enter_context(tc.tile_pool(name="const", bufs=1))
+        sg_pool = ctx.enter_context(tc.tile_pool(name="sg_pool", bufs=3))
         gate_pool = ctx.enter_context(tc.tile_pool(name="gate_pool", bufs=3))
         mx_pool = ctx.enter_context(tc.tile_pool(name="mx_pool", bufs=2))
-        y_pool = ctx.enter_context(tc.tile_pool(name="y_pool", bufs=4))
-        o_pool = ctx.enter_context(tc.tile_pool(name="o_pool", bufs=2 * GROUP))
-        stat_pool = ctx.enter_context(tc.tile_pool(name="stat_pool", bufs=2))
+        y_pool = ctx.enter_context(tc.tile_pool(name="y_pool", bufs=3))
+        o_pool = ctx.enter_context(tc.tile_pool(name="o_pool", bufs=GROUP + 3))
+        stat_pool = ctx.enter_context(tc.tile_pool(name="stat_pool", bufs=3))
         flip_psum = ctx.enter_context(tc.psum_pool(name="flip_psum", bufs=2))
         dv_psum = ctx.enter_context(tc.psum_pool(name="dv_psum", bufs=4))
+        ctx.enter_context(tc.manual_schedule())
 
         s_dram = s.rearrange("(p i) c -> p i c", i=TILES)
         g_dram = g_v.rearrange("(p i) m -> p i m", i=TILES)
@@ -46,7 +48,6 @@ def tile_selfinteraction_pb_t_kernel(tc, s, v, g_v, wv, ln_g1, out):
         out_dram = out.rearrange("(p i) c d -> p i c d", i=TILES)
 
         wv_rows = const.tile([P, PACK, C], BF16)
-        nc.sync.dma_start(out=wv_rows[:], in_=wv.rearrange("(t p) c -> p t c", p=P))
         s_sb = const.tile([P, TILES, C], BF16)
         g_sb = const.tile([P, TILES, KV], BF16)
         v_sb = const.tile([P, TILES, C, DIMS], BF16)
@@ -57,6 +58,7 @@ def tile_selfinteraction_pb_t_kernel(tc, s, v, g_v, wv, ln_g1, out):
             nc.sync.dma_start(out=g_sb[:, rows, :], in_=g_dram[:, rows, :])
             nc.sync.dma_start(out=v_sb[:, rows, :, :], in_=v_dram[:, rows, :, :])
             if g == 0:
+                nc.sync.dma_start(out=wv_rows[:], in_=wv.rearrange("(t p) c -> p t c", p=P))
                 nc.sync.dma_start(out=gain_sb[:], in_=ln_g1.partition_broadcast(P))
 
         ident_bf16 = const.tile([P, P], BF16)
@@ -65,6 +67,159 @@ def tile_selfinteraction_pb_t_kernel(tc, s, v, g_v, wv, ln_g1, out):
         make_identity(nc, ident_f32[:])
         eps_sb = const.tile([P, 1], F32)
         nc.vector.memset(eps_sb[:], EPS)
+
+        sg_of = {}
+        vg_t_of = {}
+        sg_t_of = {}
+        gates_of = {}
+        u_grouped_of = {}
+        u_codes_of = {}
+        u_scales_of = {}
+        dv_of = {}
+        y_of = {}
+        o_of = {}
+        sum_sq_of = {}
+        rms_of = {}
+        inv_rms_of = {}
+
+        def scalar_gates(g):
+            rows = slice(g * GROUP, (g + 1) * GROUP)
+            sg = sg_pool.tile([P, GROUP, C], F32, tag="sg")
+            nc.gpsimd.tensor_tensor(out=sg[:], in0=s_sb[:, rows, :], in1=g_sb[:, rows, C:KV], op=MULT)
+            sg_of[g] = sg
+
+        def flip(i):
+            vg_t = flip_psum.tile([P, 2 * DIMS + HALVES, P], BF16, tag="vg_t")
+            sg_t = flip_psum.tile([P, HALVES, P], F32, tag="sg_t")
+            for j in range(HALVES):
+                cols = slice(j * P, (j + 1) * P)
+                nc.tensor.transpose(
+                    out=sg_t[:, j, :], in_=sg_of[i // GROUP][:, i % GROUP, cols], identity=ident_f32[:]
+                )
+            for j in range(HALVES):
+                cols = slice(j * P, (j + 1) * P)
+                nc.tensor.transpose(
+                    out=vg_t[:, 2 * DIMS + j, :], in_=g_sb[:, i, cols], identity=ident_bf16[:]
+                )
+                for d in range(DIMS):
+                    nc.tensor.transpose(
+                        out=vg_t[:, DIMS * j + d, :], in_=v_sb[:, i, cols, d], identity=ident_bf16[:]
+                    )
+            vg_t_of[i] = vg_t
+            sg_t_of[i] = sg_t
+
+        def fetch_gates(i):
+            gates = gate_pool.tile([P, 2, P, HALVES], F32, tag="gates")
+            nc.scalar.copy(
+                out=gates[:, 0, :, :],
+                in_=vg_t_of[i][:, 2 * DIMS : 2 * DIMS + HALVES, :].rearrange("p j n -> p n j"),
+            )
+            nc.scalar.mul(
+                out=gates[:, 1, :, :], in_=sg_t_of[i][:].rearrange("p j n -> p n j"), mul=math.sqrt(2.0)
+            )
+            gates_of[i] = gates
+
+        def gate_product(i):
+            g, k = divmod(i, GROUP)
+            if k == 0:
+                u_grouped = mx_pool.tile(
+                    [P, DIMS, GROUP, P, PACK], BF16, align_bytes=64, tag="u_grouped"
+                )
+                u_grouped_of[g] = u_grouped
+            v_t = vg_t_of[i][:, 0 : 2 * DIMS, :].rearrange("p (j d) n -> p d n j", d=DIMS)
+            for d in range(DIMS):
+                nc.vector.tensor_tensor(
+                    out=u_grouped_of[g][:, d, k, :, :].rearrange("p n (h j) -> p n h j", j=HALVES),
+                    in0=v_t[:, d, :, :].unsqueeze(2).to_broadcast([P, P, 2, HALVES]),
+                    in1=gates_of[i][:].rearrange("p h n j -> p n h j"),
+                    op=MULT,
+                )
+
+        def quantise(g):
+            u_codes = mx_pool.tile([P, DIMS, GROUP * P], U32, align_bytes=64, tag="u_codes")
+            u_scales = mx_pool.tile([P, DIMS, GROUP * P], U8, align_bytes=64, tag="u_scales")
+            for d in range(DIMS):
+                nc.vector.quantize_mx(
+                    out=u_codes[:, d, :].bitcast(FP8X4),
+                    scales=u_scales[:, d, :],
+                    in_=u_grouped_of[g][:, d, :, :, :].rearrange("p k n t -> p (k n t)"),
+                )
+            u_codes_of[g] = u_codes
+            u_scales_of[g] = u_scales
+
+        def project(i):
+            g, k = divmod(i, GROUP)
+            points = slice(k * P, (k + 1) * P)
+            for half in range(HALVES):
+                cols = slice(half * P, (half + 1) * P)
+                dv = dv_psum.tile([P, DIMS, P], F32, tag="dv")
+                for d in range(DIMS):
+                    nc.tensor.matmul_mx(
+                        out=dv[:, d, :],
+                        lhsT=u_codes_of[g][:, d, points].bitcast(FP8X4),
+                        lhsT_scale=u_scales_of[g][:, d, points],
+                        rhs=wv_codes[:, cols].bitcast(FP8X4),
+                        rhs_scale=wv_scales[:, cols],
+                        start=True,
+                        stop=True,
+                    )
+                dv_of[(i, half)] = dv
+
+        def residual(i):
+            y = y_pool.tile([P, C, DIMS], F32, tag="y")
+            for half in range(HALVES):
+                cols = slice(half * P, (half + 1) * P)
+                nc.vector.scalar_tensor_tensor(
+                    out=y[:, cols, :],
+                    in0=dv_of[(i, half)][:].rearrange("p d c -> p c d"),
+                    scalar=1.0 / math.sqrt(KV),
+                    in1=v_sb[:, i, cols, :],
+                    op0=MULT,
+                    op1=ADD,
+                )
+            y_of[i] = y
+
+        def sum_squares(i):
+            g, k = divmod(i, GROUP)
+            if k == 0:
+                sum_sq = stat_pool.tile([P, GROUP], F32, tag="sum_sq")
+                sum_sq_of[g] = sum_sq
+            squares = y_pool.tile([P, C, DIMS], BF16, tag="squares")
+            nc.scalar.activation(
+                out=squares[:], in_=y_of[i][:], func=ACT.Square, accum_out=sum_sq_of[g][:, k : k + 1]
+            )
+
+        def apply_gain(i):
+            o = o_pool.tile([P, C, DIMS], F32, tag="o")
+            nc.gpsimd.tensor_tensor(
+                out=o[:], in0=y_of[i][:], in1=gain_sb[:].unsqueeze(2).to_broadcast([P, C, DIMS]), op=MULT
+            )
+            o_of[i] = o
+
+        def root_mean_square(g):
+            rms = stat_pool.tile([P, GROUP], F32, tag="rms")
+            nc.scalar.activation(
+                out=rms[:], in_=sum_sq_of[g][:], func=ACT.Sqrt, bias=eps_sb[:], scale=1.0 / (C * DIMS)
+            )
+            rms_of[g] = rms
+
+        def invert_rms(g):
+            inv_rms = stat_pool.tile([P, GROUP], F32, tag="inv_rms")
+            nc.vector.reciprocal(out=inv_rms[:], in_=rms_of[g][:])
+            inv_rms_of[g] = inv_rms
+
+        def normalise_and_store(i):
+            g, k = divmod(i, GROUP)
+            o = o_of[i]
+            nc.scalar.activation(out=o[:], in_=o[:], func=ACT.Copy, scale=inv_rms_of[g][:, k : k + 1])
+            nc.sync.dma_start(out=out_dram[:, i, :, :], in_=o[:])
+
+        scalar_gates(0)
+        scalar_gates(1)
+        flip(0)
+        fetch_gates(0)
+        flip(1)
+        fetch_gates(1)
 
         wv_grouped = const.tile([P, C, PACK], BF16, align_bytes=64)
         nc.vector.tensor_copy(out=wv_grouped[:], in_=wv_rows[:].rearrange("p t c -> p c t"))
@@ -76,98 +231,28 @@ def tile_selfinteraction_pb_t_kernel(tc, s, v, g_v, wv, ln_g1, out):
             in_=wv_grouped[:].rearrange("p c t -> p (c t)"),
         )
 
-        def gated_tile(i, u_grouped, k):
-            sg = gate_pool.tile([P, C], F32, tag="sg")
-            nc.gpsimd.tensor_tensor(out=sg[:], in0=s_sb[:, i, :], in1=g_sb[:, i, C:KV], op=MULT)
-            vg_t = flip_psum.tile([P, 2 * DIMS + 2, P], BF16, tag="vg_t")
-            for j in range(HALVES):
-                cols = slice(j * P, (j + 1) * P)
-                for d in range(DIMS):
-                    nc.tensor.transpose(
-                        out=vg_t[:, DIMS * j + d, :], in_=v_sb[:, i, cols, d], identity=ident_bf16[:]
-                    )
-                nc.tensor.transpose(
-                    out=vg_t[:, 2 * DIMS + j, :], in_=g_sb[:, i, cols], identity=ident_bf16[:]
-                )
-            sg_t = flip_psum.tile([P, HALVES, P], F32, tag="sg_t")
-            for j in range(HALVES):
-                cols = slice(j * P, (j + 1) * P)
-                nc.tensor.transpose(out=sg_t[:, j, :], in_=sg[:, cols], identity=ident_f32[:])
-            gates = gate_pool.tile([P, 2, P, HALVES], F32, tag="gates")
-            nc.scalar.copy(
-                out=gates[:, 0, :, :],
-                in_=vg_t[:, 2 * DIMS : 2 * DIMS + HALVES, :].rearrange("p j n -> p n j"),
-            )
-            nc.scalar.mul(
-                out=gates[:, 1, :, :], in_=sg_t[:].rearrange("p j n -> p n j"), mul=math.sqrt(2.0)
-            )
-            v_t = vg_t[:, 0 : 2 * DIMS, :].rearrange("p (j d) n -> p d n j", d=DIMS)
-            for d in range(DIMS):
-                nc.vector.tensor_tensor(
-                    out=u_grouped[:, d, k, :, :].rearrange("p n (h j) -> p n h j", j=HALVES),
-                    in0=v_t[:, d, :, :].unsqueeze(2).to_broadcast([P, P, 2, HALVES]),
-                    in1=gates[:].rearrange("p h n j -> p n h j"),
-                    op=MULT,
-                )
-
-        for g in range(GROUPS):
-            u_grouped = mx_pool.tile([P, DIMS, GROUP, P, PACK], BF16, align_bytes=64, tag="u_grouped")
-            for k in range(GROUP):
-                gated_tile(g * GROUP + k, u_grouped, k)
-
-            u_codes = mx_pool.tile([P, DIMS, GROUP * P], U32, align_bytes=64, tag="u_codes")
-            u_scales = mx_pool.tile([P, DIMS, GROUP * P], U8, align_bytes=64, tag="u_scales")
-            for d in range(DIMS):
-                nc.vector.quantize_mx(
-                    out=u_codes[:, d, :].bitcast(FP8X4),
-                    scales=u_scales[:, d, :],
-                    in_=u_grouped[:, d, :, :, :].rearrange("p k n t -> p (k n t)"),
-                )
-
-            sum_sq = stat_pool.tile([P, GROUP], F32, tag="sum_sq")
-            scaled = []
-            for k in range(GROUP):
-                i = g * GROUP + k
-                points = slice(k * P, (k + 1) * P)
-                y = y_pool.tile([P, C, DIMS], F32, tag="y")
-                for half in range(HALVES):
-                    cols = slice(half * P, (half + 1) * P)
-                    dv = dv_psum.tile([P, DIMS, P], F32, tag="dv")
-                    for d in range(DIMS):
-                        nc.tensor.matmul_mx(
-                            out=dv[:, d, :],
-                            lhsT=u_codes[:, d, points].bitcast(FP8X4),
-                            lhsT_scale=u_scales[:, d, points],
-                            rhs=wv_codes[:, cols].bitcast(FP8X4),
-                            rhs_scale=wv_scales[:, cols],
-                            start=True,
-                            stop=True,
-                        )
-                    nc.vector.scalar_tensor_tensor(
-                        out=y[:, cols, :],
-                        in0=dv[:].rearrange("p d c -> p c d"),
-                        scalar=1.0 / math.sqrt(KV),
-                        in1=v_sb[:, i, cols, :],
-                        op0=MULT,
-                        op1=ADD,
-                    )
-                squares = y_pool.tile([P, C, DIMS], BF16, tag="squares")
-                nc.scalar.activation(
-                    out=squares[:], in_=y[:], func=ACT.Square, accum_out=sum_sq[:, k : k + 1]
-                )
-                o = o_pool.tile([P, C, DIMS], F32, tag="o")
-                nc.gpsimd.tensor_tensor(
-                    out=o[:], in0=y[:], in1=gain_sb[:].unsqueeze(2).to_broadcast([P, C, DIMS]), op=MULT
-                )
-                scaled.append(o)
-
-            rms = stat_pool.tile([P, GROUP], F32, tag="rms")
-            nc.scalar.activation(
-                out=rms[:], in_=sum_sq[:], func=ACT.Sqrt, bias=eps_sb[:], scale=1.0 / (C * DIMS)
-            )
-            inv_rms = stat_pool.tile([P, GROUP], F32, tag="inv_rms")
-            nc.vector.reciprocal(out=inv_rms[:], in_=rms[:])
-            for k in range(GROUP):
-                o = scaled[k]
-                nc.scalar.activation(out=o[:], in_=o[:], func=ACT.Copy, scale=inv_rms[:, k : k + 1])
-                nc.sync.dma_start(out=out_dram[:, g * GROUP + k, :, :], in_=o[:])
+        for a in range(TILES + 2 * GROUP + 2):
+            b = a - GROUP - 1
+            z = a - 2 * GROUP - 2
+            if a % GROUP == 0 and a // GROUP + 2 < GROUPS:
+                scalar_gates(a // GROUP + 2)
+            if 0 <= b < TILES:
+                project(b)
+            if a < TILES:
+                gate_product(a)
+            if a % GROUP == 0 and 1 <= a // GROUP <= GROUPS:
+                quantise(a // GROUP - 1)
+            if b % GROUP == 0 and 1 <= b // GROUP <= GROUPS:
+                invert_rms(b // GROUP - 1)
+            if a + 2 < TILES:
+                flip(a + 2)
+            if 0 <= b < TILES:
+                residual(b)
+                sum_squares(b)
+                if b % GROUP == GROUP - 1:
+                    root_mean_square(b // GROUP)
+                apply_gain(b)
+            if a + 2 < TILES:
+                fetch_gates(a + 2)
+            if 0 <= z < TILES:
+                normalise_and_store(z)

@@ -50,7 +50,8 @@ def tile_selfinteraction_pb_t_kernel(tc, s, v, g_v, wv, ln_g1, out):
         wv_rows = const.tile([P, PACK, C], BF16)
         s_sb = const.tile([P, TILES, C], BF16)
         g_sb = const.tile([P, TILES, KV], BF16)
-        v_sb = const.tile([P, TILES, C, DIMS], BF16)
+        v_flat = const.tile([P, TILES, C * DIMS], BF16)
+        v_sb = v_flat[:].rearrange("p i (c d) -> p i c d", d=DIMS)
         gain_sb = const.tile([P, C], BF16)
         for g in range(GROUPS):
             rows = slice(g * GROUP, (g + 1) * GROUP)
@@ -58,15 +59,19 @@ def tile_selfinteraction_pb_t_kernel(tc, s, v, g_v, wv, ln_g1, out):
             nc.sync.dma_start(out=g_sb[:, rows, :], in_=g_dram[:, rows, :])
             nc.sync.dma_start(out=v_sb[:, rows, :, :], in_=v_dram[:, rows, :, :])
             if g == 0:
-                nc.sync.dma_start(out=wv_rows[:], in_=wv.rearrange("(t p) c -> p t c", p=P))
+                nc.sync.dma_start(
+                    out=wv_rows[:].rearrange("q (h e) c -> q h e c", e=2),
+                    in_=wv.rearrange("(h q e) c -> q h e c", h=2, e=2),
+                )
                 nc.sync.dma_start(out=gain_sb[:], in_=ln_g1.partition_broadcast(P))
 
-        ident_bf16 = const.tile([P, P], BF16)
-        make_identity(nc, ident_bf16[:])
         ident_f32 = const.tile([P, P], F32)
         make_identity(nc, ident_f32[:])
         eps_sb = const.tile([P, 1], F32)
         nc.vector.memset(eps_sb[:], EPS)
+
+        v_words = v_flat[:].bitcast(F32)
+        g_words = g_sb[:].bitcast(F32)
 
         sg_of = {}
         vg_t_of = {}
@@ -84,40 +89,47 @@ def tile_selfinteraction_pb_t_kernel(tc, s, v, g_v, wv, ln_g1, out):
 
         def scalar_gates(g):
             rows = slice(g * GROUP, (g + 1) * GROUP)
-            sg = sg_pool.tile([P, GROUP, C], F32, tag="sg")
-            nc.gpsimd.tensor_tensor(out=sg[:], in0=s_sb[:, rows, :], in1=g_sb[:, rows, C:KV], op=MULT)
+            sg = sg_pool.tile([P, GROUP, 2, P], F32, tag="sg")
+            nc.gpsimd.tensor_tensor(
+                out=sg[:],
+                in0=s_sb[:, rows, :].rearrange("p k (q e) -> p k e q", e=2),
+                in1=g_sb[:, rows, C:KV].rearrange("p k (q e) -> p k e q", e=2),
+                op=MULT,
+            )
             sg_of[g] = sg
 
         def flip(i):
-            vg_t = flip_psum.tile([P, 2 * DIMS + HALVES, P], BF16, tag="vg_t")
-            sg_t = flip_psum.tile([P, HALVES, P], F32, tag="sg_t")
-            for j in range(HALVES):
-                cols = slice(j * P, (j + 1) * P)
+            vg_t = flip_psum.tile([P, (DIMS + 1) * P], F32, tag="vg_t")
+            for r in range(DIMS):
                 nc.tensor.transpose(
-                    out=sg_t[:, j, :], in_=sg_of[i // GROUP][:, i % GROUP, cols], identity=ident_f32[:]
+                    out=vg_t[:, r * P : (r + 1) * P],
+                    in_=v_words[:, i, r : DIMS * P : DIMS],
+                    identity=ident_f32[:],
                 )
-            for j in range(HALVES):
-                cols = slice(j * P, (j + 1) * P)
+            nc.tensor.transpose(
+                out=vg_t[:, DIMS * P : (DIMS + 1) * P], in_=g_words[:, i, 0:P], identity=ident_f32[:]
+            )
+            sg_t = flip_psum.tile([P, 2, P], F32, tag="sg_t")
+            for e in range(2):
                 nc.tensor.transpose(
-                    out=vg_t[:, 2 * DIMS + j, :], in_=g_sb[:, i, cols], identity=ident_bf16[:]
+                    out=sg_t[:, e, :], in_=sg_of[i // GROUP][:, i % GROUP, e, :], identity=ident_f32[:]
                 )
-                for d in range(DIMS):
-                    nc.tensor.transpose(
-                        out=vg_t[:, DIMS * j + d, :], in_=v_sb[:, i, cols, d], identity=ident_bf16[:]
-                    )
             vg_t_of[i] = vg_t
             sg_t_of[i] = sg_t
 
         def fetch_gates(i):
-            gates = gate_pool.tile([P, 2, P, HALVES], F32, tag="gates")
+            gates = gate_pool.tile([P, 2, P, 2], F32, tag="gates")
             nc.scalar.copy(
                 out=gates[:, 0, :, :],
-                in_=vg_t_of[i][:, 2 * DIMS : 2 * DIMS + HALVES, :].rearrange("p j n -> p n j"),
+                in_=vg_t_of[i][:, DIMS * P : (DIMS + 1) * P].bitcast(BF16).rearrange("q (n e) -> q n e", e=2),
             )
             nc.scalar.mul(
-                out=gates[:, 1, :, :], in_=sg_t_of[i][:].rearrange("p j n -> p n j"), mul=math.sqrt(2.0)
+                out=gates[:, 1, :, :], in_=sg_t_of[i][:].rearrange("q e n -> q n e"), mul=math.sqrt(2.0)
             )
             gates_of[i] = gates
+
+        def place(f):
+            return 2 * P * (f // 2) + f % 2
 
         def gate_product(i):
             g, k = divmod(i, GROUP)
@@ -126,12 +138,18 @@ def tile_selfinteraction_pb_t_kernel(tc, s, v, g_v, wv, ln_g1, out):
                     [P, DIMS, GROUP, P, PACK], BF16, align_bytes=64, tag="u_grouped"
                 )
                 u_grouped_of[g] = u_grouped
-            v_t = vg_t_of[i][:, 0 : 2 * DIMS, :].rearrange("p (j d) n -> p d n j", d=DIMS)
+            halves = vg_t_of[i][:].bitcast(BF16)
             for d in range(DIMS):
+                first = place(d)
+                apart = place(DIMS + d) - first
+                v_pair = halves[:, first : first + 2 * apart].rearrange("q (e w) -> q e w", e=2)
                 nc.vector.tensor_tensor(
-                    out=u_grouped_of[g][:, d, k, :, :].rearrange("p n (h j) -> p n h j", j=HALVES),
-                    in0=v_t[:, d, :, :].unsqueeze(2).to_broadcast([P, P, 2, HALVES]),
-                    in1=gates_of[i][:].rearrange("p h n j -> p n h j"),
+                    out=u_grouped_of[g][:, d, k, :, :].rearrange("q n (h e) -> q n h e", e=2),
+                    in0=v_pair[:, :, 0 : 2 * P : 2]
+                    .rearrange("q e n -> q n e")
+                    .unsqueeze(2)
+                    .to_broadcast([P, P, 2, 2]),
+                    in1=gates_of[i][:].rearrange("q h n e -> q n h e"),
                     op=MULT,
                 )
 

@@ -35,8 +35,8 @@ def tile_selfinteraction_pb_t_kernel(tc, s, v, g_v, wv, ln_g1, out):
         sg_pool = ctx.enter_context(tc.tile_pool(name="sg_pool", bufs=3))
         gate_pool = ctx.enter_context(tc.tile_pool(name="gate_pool", bufs=3))
         mx_pool = ctx.enter_context(tc.tile_pool(name="mx_pool", bufs=2))
-        y_pool = ctx.enter_context(tc.tile_pool(name="y_pool", bufs=3))
-        o_pool = ctx.enter_context(tc.tile_pool(name="o_pool", bufs=GROUP + 3))
+        y_pool = ctx.enter_context(tc.tile_pool(name="y_pool", bufs=5))
+        o_pool = ctx.enter_context(tc.tile_pool(name="o_pool", bufs=GROUP + 6))
         stat_pool = ctx.enter_context(tc.tile_pool(name="stat_pool", bufs=3))
         flip_psum = ctx.enter_context(tc.psum_pool(name="flip_psum", bufs=2))
         dv_psum = ctx.enter_context(tc.psum_pool(name="dv_psum", bufs=4))
@@ -69,6 +69,8 @@ def tile_selfinteraction_pb_t_kernel(tc, s, v, g_v, wv, ln_g1, out):
         make_identity(nc, ident_f32[:])
         eps_sb = const.tile([P, 1], F32)
         nc.vector.memset(eps_sb[:], EPS)
+        table_warmer = const.tile([P, 1], F32)
+        nc.scalar.sqrt(out=table_warmer[:], in_=eps_sb[:])
 
         v_words = v_flat[:].bitcast(F32)
         g_words = g_sb[:].bitcast(F32)
@@ -252,24 +254,25 @@ def tile_selfinteraction_pb_t_kernel(tc, s, v, g_v, wv, ln_g1, out):
         for a in range(TILES + 2 * GROUP + 2):
             b = a - GROUP - 1
             z = a - 2 * GROUP - 2
-            if a % GROUP == 0 and a // GROUP + 2 < GROUPS:
-                scalar_gates(a // GROUP + 2)
             if 0 <= b < TILES:
                 project(b)
             if a < TILES:
                 gate_product(a)
-            if a % GROUP == 0 and 1 <= a // GROUP <= GROUPS:
-                quantise(a // GROUP - 1)
             if b % GROUP == 0 and 1 <= b // GROUP <= GROUPS:
                 invert_rms(b // GROUP - 1)
             if a + 2 < TILES:
                 flip(a + 2)
             if 0 <= b < TILES:
                 residual(b)
+            if a % GROUP == 0 and 1 <= a // GROUP <= GROUPS:
+                quantise(a // GROUP - 1)
+            if 0 <= b < TILES:
                 sum_squares(b)
                 if b % GROUP == GROUP - 1:
                     root_mean_square(b // GROUP)
                 apply_gain(b)
+            if a % GROUP == 0 and a // GROUP + 2 < GROUPS:
+                scalar_gates(a // GROUP + 2)
             if a + 2 < TILES:
                 fetch_gates(a + 2)
             if 0 <= z < TILES:

@@ -19,10 +19,12 @@ C = 256
 DIMS = 3
 KV = 2 * C
 PACK = 4
+PAIR = 2
 TILES = POINTS // P
 GROUP = 2
 GROUPS = TILES // GROUP
-HALVES = C // P
+C_BLOCKS = C // P
+AHEAD = 2
 EPS = 1e-6
 
 FLOPS = 2 * POINTS * DIMS * KV * C
@@ -33,47 +35,47 @@ def tile_selfinteraction_pb_t_kernel(tc, s, v, g_v, wv, ln_g1, out):
     with ExitStack() as ctx:
         const = ctx.enter_context(tc.tile_pool(name="const", bufs=1))
         sg_pool = ctx.enter_context(tc.tile_pool(name="sg_pool", bufs=3))
-        gate_pool = ctx.enter_context(tc.tile_pool(name="gate_pool", bufs=3))
+        gate_pool = ctx.enter_context(tc.tile_pool(name="gate_pool", bufs=AHEAD + 1))
         mx_pool = ctx.enter_context(tc.tile_pool(name="mx_pool", bufs=2))
         y_pool = ctx.enter_context(tc.tile_pool(name="y_pool", bufs=5))
-        o_pool = ctx.enter_context(tc.tile_pool(name="o_pool", bufs=GROUP + 6))
+        o_pool = ctx.enter_context(tc.tile_pool(name="o_pool", bufs=GROUP + 5))
         stat_pool = ctx.enter_context(tc.tile_pool(name="stat_pool", bufs=3))
-        flip_psum = ctx.enter_context(tc.psum_pool(name="flip_psum", bufs=2))
-        dv_psum = ctx.enter_context(tc.psum_pool(name="dv_psum", bufs=4))
+        flip_psum = ctx.enter_context(tc.psum_pool(name="flip_psum", bufs=AHEAD))
+        dv_psum = ctx.enter_context(tc.psum_pool(name="dv_psum", bufs=2 * C_BLOCKS))
         ctx.enter_context(tc.manual_schedule())
 
         s_dram = s.rearrange("(p i) c -> p i c", i=TILES)
         g_dram = g_v.rearrange("(p i) m -> p i m", i=TILES)
-        v_dram = v.rearrange("(p i) c d -> p i c d", i=TILES)
+        v_dram = v.rearrange("(p i) c d -> p i (c d)", i=TILES)
         out_dram = out.rearrange("(p i) c d -> p i c d", i=TILES)
 
-        wv_rows = const.tile([P, PACK, C], BF16)
         s_sb = const.tile([P, TILES, C], BF16)
         g_sb = const.tile([P, TILES, KV], BF16)
-        v_flat = const.tile([P, TILES, C * DIMS], BF16)
-        v_sb = v_flat[:].rearrange("p i (c d) -> p i c d", d=DIMS)
+        v_sb = const.tile([P, TILES, C * DIMS], BF16)
+        wv_rows = const.tile([P, PACK, C], BF16)
         gain_sb = const.tile([P, C], BF16)
         for g in range(GROUPS):
-            rows = slice(g * GROUP, (g + 1) * GROUP)
-            nc.sync.dma_start(out=s_sb[:, rows, :], in_=s_dram[:, rows, :])
-            nc.sync.dma_start(out=g_sb[:, rows, :], in_=g_dram[:, rows, :])
-            nc.sync.dma_start(out=v_sb[:, rows, :, :], in_=v_dram[:, rows, :, :])
+            tiles = slice(g * GROUP, (g + 1) * GROUP)
+            nc.sync.dma_start(out=s_sb[:, tiles, :], in_=s_dram[:, tiles, :])
+            nc.sync.dma_start(out=g_sb[:, tiles, :], in_=g_dram[:, tiles, :])
+            nc.sync.dma_start(out=v_sb[:, tiles, :], in_=v_dram[:, tiles, :])
             if g == 0:
                 nc.sync.dma_start(
-                    out=wv_rows[:].rearrange("q (h e) c -> q h e c", e=2),
-                    in_=wv.rearrange("(h q e) c -> q h e c", h=2, e=2),
+                    out=wv_rows[:].rearrange("q (h e) c -> q h e c", e=PAIR),
+                    in_=wv.rearrange("(h q e) c -> q h e c", h=2, e=PAIR),
                 )
                 nc.sync.dma_start(out=gain_sb[:], in_=ln_g1.partition_broadcast(P))
 
-        ident_f32 = const.tile([P, P], F32)
-        make_identity(nc, ident_f32[:])
+        v_words = v_sb[:].bitcast(F32)
+        g_words = g_sb[:].bitcast(F32)
+        v_cd = v_sb[:].rearrange("p i (c d) -> p i c d", d=DIMS)
+
+        ident = const.tile([P, P], F32)
+        make_identity(nc, ident[:])
         eps_sb = const.tile([P, 1], F32)
         nc.vector.memset(eps_sb[:], EPS)
         table_warmer = const.tile([P, 1], F32)
-        nc.scalar.sqrt(out=table_warmer[:], in_=eps_sb[:])
-
-        v_words = v_flat[:].bitcast(F32)
-        g_words = g_sb[:].bitcast(F32)
+        nc.scalar.activation(out=table_warmer[:], in_=eps_sb[:], func=ACT.Abs_reciprocal_sqrt)
 
         sg_of = {}
         vg_t_of = {}
@@ -86,16 +88,15 @@ def tile_selfinteraction_pb_t_kernel(tc, s, v, g_v, wv, ln_g1, out):
         y_of = {}
         o_of = {}
         sum_sq_of = {}
-        rms_of = {}
         inv_rms_of = {}
 
         def scalar_gates(g):
-            rows = slice(g * GROUP, (g + 1) * GROUP)
-            sg = sg_pool.tile([P, GROUP, 2, P], F32, tag="sg")
+            tiles = slice(g * GROUP, (g + 1) * GROUP)
+            sg = sg_pool.tile([P, GROUP, PAIR, P], F32, tag="sg")
             nc.gpsimd.tensor_tensor(
                 out=sg[:],
-                in0=s_sb[:, rows, :].rearrange("p k (q e) -> p k e q", e=2),
-                in1=g_sb[:, rows, C:KV].rearrange("p k (q e) -> p k e q", e=2),
+                in0=s_sb[:, tiles, :].rearrange("p k (q e) -> p k e q", e=PAIR),
+                in1=g_sb[:, tiles, C:KV].rearrange("p k (q e) -> p k e q", e=PAIR),
                 op=MULT,
             )
             sg_of[g] = sg
@@ -106,24 +107,26 @@ def tile_selfinteraction_pb_t_kernel(tc, s, v, g_v, wv, ln_g1, out):
                 nc.tensor.transpose(
                     out=vg_t[:, r * P : (r + 1) * P],
                     in_=v_words[:, i, r : DIMS * P : DIMS],
-                    identity=ident_f32[:],
+                    identity=ident[:],
                 )
             nc.tensor.transpose(
-                out=vg_t[:, DIMS * P : (DIMS + 1) * P], in_=g_words[:, i, 0:P], identity=ident_f32[:]
+                out=vg_t[:, DIMS * P : (DIMS + 1) * P], in_=g_words[:, i, 0:P], identity=ident[:]
             )
-            sg_t = flip_psum.tile([P, 2, P], F32, tag="sg_t")
-            for e in range(2):
+            sg_t = flip_psum.tile([P, PAIR, P], F32, tag="sg_t")
+            for e in range(PAIR):
                 nc.tensor.transpose(
-                    out=sg_t[:, e, :], in_=sg_of[i // GROUP][:, i % GROUP, e, :], identity=ident_f32[:]
+                    out=sg_t[:, e, :], in_=sg_of[i // GROUP][:, i % GROUP, e, :], identity=ident[:]
                 )
             vg_t_of[i] = vg_t
             sg_t_of[i] = sg_t
 
         def fetch_gates(i):
-            gates = gate_pool.tile([P, 2, P, 2], F32, tag="gates")
+            gates = gate_pool.tile([P, 2, P, PAIR], F32, tag="gates")
             nc.scalar.copy(
                 out=gates[:, 0, :, :],
-                in_=vg_t_of[i][:, DIMS * P : (DIMS + 1) * P].bitcast(BF16).rearrange("q (n e) -> q n e", e=2),
+                in_=vg_t_of[i][:, DIMS * P : (DIMS + 1) * P]
+                .bitcast(BF16)
+                .rearrange("q (n e) -> q n e", e=PAIR),
             )
             nc.scalar.mul(
                 out=gates[:, 1, :, :], in_=sg_t_of[i][:].rearrange("q e n -> q n e"), mul=math.sqrt(2.0)
@@ -131,7 +134,7 @@ def tile_selfinteraction_pb_t_kernel(tc, s, v, g_v, wv, ln_g1, out):
             gates_of[i] = gates
 
         def place(f):
-            return 2 * P * (f // 2) + f % 2
+            return PAIR * P * (f // PAIR) + f % PAIR
 
         def gate_product(i):
             g, k = divmod(i, GROUP)
@@ -144,13 +147,13 @@ def tile_selfinteraction_pb_t_kernel(tc, s, v, g_v, wv, ln_g1, out):
             for d in range(DIMS):
                 first = place(d)
                 apart = place(DIMS + d) - first
-                v_pair = halves[:, first : first + 2 * apart].rearrange("q (e w) -> q e w", e=2)
+                v_pair = halves[:, first : first + PAIR * apart].rearrange("q (e w) -> q e w", e=PAIR)
                 nc.vector.tensor_tensor(
-                    out=u_grouped_of[g][:, d, k, :, :].rearrange("q n (h e) -> q n h e", e=2),
-                    in0=v_pair[:, :, 0 : 2 * P : 2]
+                    out=u_grouped_of[g][:, d, k, :, :].rearrange("q n (h e) -> q n h e", e=PAIR),
+                    in0=v_pair[:, :, 0 : PAIR * P : PAIR]
                     .rearrange("q e n -> q n e")
                     .unsqueeze(2)
-                    .to_broadcast([P, P, 2, 2]),
+                    .to_broadcast([P, P, 2, PAIR]),
                     in1=gates_of[i][:].rearrange("q h n e -> q n h e"),
                     op=MULT,
                 )
@@ -162,7 +165,7 @@ def tile_selfinteraction_pb_t_kernel(tc, s, v, g_v, wv, ln_g1, out):
                 nc.vector.quantize_mx(
                     out=u_codes[:, d, :].bitcast(FP8X4),
                     scales=u_scales[:, d, :],
-                    in_=u_grouped_of[g][:, d, :, :, :].rearrange("p k n t -> p (k n t)"),
+                    in_=u_grouped_of[g][:, d, :, :, :].rearrange("q k n t -> q (k n t)"),
                 )
             u_codes_of[g] = u_codes
             u_scales_of[g] = u_scales
@@ -170,8 +173,8 @@ def tile_selfinteraction_pb_t_kernel(tc, s, v, g_v, wv, ln_g1, out):
         def project(i):
             g, k = divmod(i, GROUP)
             points = slice(k * P, (k + 1) * P)
-            for half in range(HALVES):
-                cols = slice(half * P, (half + 1) * P)
+            for block in range(C_BLOCKS):
+                cols = slice(block * P, (block + 1) * P)
                 dv = dv_psum.tile([P, DIMS, P], F32, tag="dv")
                 for d in range(DIMS):
                     nc.tensor.matmul_mx(
@@ -183,17 +186,17 @@ def tile_selfinteraction_pb_t_kernel(tc, s, v, g_v, wv, ln_g1, out):
                         start=True,
                         stop=True,
                     )
-                dv_of[(i, half)] = dv
+                dv_of[(i, block)] = dv
 
         def residual(i):
             y = y_pool.tile([P, C, DIMS], F32, tag="y")
-            for half in range(HALVES):
-                cols = slice(half * P, (half + 1) * P)
+            for block in range(C_BLOCKS):
+                cols = slice(block * P, (block + 1) * P)
                 nc.vector.scalar_tensor_tensor(
                     out=y[:, cols, :],
-                    in0=dv_of[(i, half)][:].rearrange("p d c -> p c d"),
+                    in0=dv_of[(i, block)][:].rearrange("p d c -> p c d"),
                     scalar=1.0 / math.sqrt(KV),
-                    in1=v_sb[:, i, cols, :],
+                    in1=v_cd[:, i, cols, :],
                     op0=MULT,
                     op1=ADD,
                 )
@@ -209,24 +212,23 @@ def tile_selfinteraction_pb_t_kernel(tc, s, v, g_v, wv, ln_g1, out):
                 out=squares[:], in_=y_of[i][:], func=ACT.Square, accum_out=sum_sq_of[g][:, k : k + 1]
             )
 
+        def inverse_rms(g):
+            inv_rms = stat_pool.tile([P, GROUP], F32, tag="inv_rms")
+            nc.scalar.activation(
+                out=inv_rms[:],
+                in_=sum_sq_of[g][:],
+                func=ACT.Abs_reciprocal_sqrt,
+                bias=eps_sb[:],
+                scale=1.0 / (C * DIMS),
+            )
+            inv_rms_of[g] = inv_rms
+
         def apply_gain(i):
             o = o_pool.tile([P, C, DIMS], F32, tag="o")
             nc.gpsimd.tensor_tensor(
                 out=o[:], in0=y_of[i][:], in1=gain_sb[:].unsqueeze(2).to_broadcast([P, C, DIMS]), op=MULT
             )
             o_of[i] = o
-
-        def root_mean_square(g):
-            rms = stat_pool.tile([P, GROUP], F32, tag="rms")
-            nc.scalar.activation(
-                out=rms[:], in_=sum_sq_of[g][:], func=ACT.Sqrt, bias=eps_sb[:], scale=1.0 / (C * DIMS)
-            )
-            rms_of[g] = rms
-
-        def invert_rms(g):
-            inv_rms = stat_pool.tile([P, GROUP], F32, tag="inv_rms")
-            nc.vector.reciprocal(out=inv_rms[:], in_=rms_of[g][:])
-            inv_rms_of[g] = inv_rms
 
         def normalise_and_store(i):
             g, k = divmod(i, GROUP)
@@ -236,44 +238,42 @@ def tile_selfinteraction_pb_t_kernel(tc, s, v, g_v, wv, ln_g1, out):
 
         scalar_gates(0)
         scalar_gates(1)
-        flip(0)
-        fetch_gates(0)
-        flip(1)
-        fetch_gates(1)
+        for i in range(AHEAD):
+            flip(i)
+            fetch_gates(i)
 
         wv_grouped = const.tile([P, C, PACK], BF16, align_bytes=64)
-        nc.vector.tensor_copy(out=wv_grouped[:], in_=wv_rows[:].rearrange("p t c -> p c t"))
+        nc.vector.tensor_copy(out=wv_grouped[:], in_=wv_rows[:].rearrange("q t c -> q c t"))
         wv_codes = const.tile([P, C], U32, align_bytes=64)
         wv_scales = const.tile([P, C], U8, align_bytes=64)
         nc.vector.quantize_mx(
             out=wv_codes[:].bitcast(FP8X4),
             scales=wv_scales[:],
-            in_=wv_grouped[:].rearrange("p c t -> p (c t)"),
+            in_=wv_grouped[:].rearrange("q c t -> q (c t)"),
         )
 
-        for a in range(TILES + 2 * GROUP + 2):
-            b = a - GROUP - 1
-            z = a - 2 * GROUP - 2
-            if 0 <= b < TILES:
-                project(b)
-            if a < TILES:
-                gate_product(a)
-            if b % GROUP == 0 and 1 <= b // GROUP <= GROUPS:
-                invert_rms(b // GROUP - 1)
-            if a + 2 < TILES:
-                flip(a + 2)
-            if 0 <= b < TILES:
-                residual(b)
-            if a % GROUP == 0 and 1 <= a // GROUP <= GROUPS:
-                quantise(a // GROUP - 1)
-            if 0 <= b < TILES:
-                sum_squares(b)
-                if b % GROUP == GROUP - 1:
-                    root_mean_square(b // GROUP)
-                apply_gain(b)
-            if a % GROUP == 0 and a // GROUP + 2 < GROUPS:
-                scalar_gates(a // GROUP + 2)
-            if a + 2 < TILES:
-                fetch_gates(a + 2)
-            if 0 <= z < TILES:
-                normalise_and_store(z)
+        for tile_u in range(TILES + 2 * GROUP + 1):
+            tile_y = tile_u - GROUP - 1
+            tile_o = tile_y - GROUP
+            starts_group = tile_u % GROUP == 0
+            if 0 <= tile_y < TILES:
+                project(tile_y)
+            if tile_u < TILES:
+                gate_product(tile_u)
+            if tile_u + AHEAD < TILES:
+                flip(tile_u + AHEAD)
+            if 0 <= tile_y < TILES:
+                residual(tile_y)
+            if starts_group and 1 <= tile_u // GROUP <= GROUPS:
+                quantise(tile_u // GROUP - 1)
+            if 0 <= tile_y < TILES:
+                sum_squares(tile_y)
+                if tile_y % GROUP == GROUP - 1:
+                    inverse_rms(tile_y // GROUP)
+                apply_gain(tile_y)
+            if starts_group and tile_u // GROUP + 2 < GROUPS:
+                scalar_gates(tile_u // GROUP + 2)
+            if tile_u + AHEAD < TILES:
+                fetch_gates(tile_u + AHEAD)
+            if 0 <= tile_o < TILES:
+                normalise_and_store(tile_o)

@@ -20,11 +20,14 @@ DIMS = 3
 KV = 2 * C
 PACK = 4
 PAIR = 2
+PARTS = 2
 TILES = POINTS // P
 GROUP = 2
 GROUPS = TILES // GROUP
-C_BLOCKS = C // P
+C_CHUNKS = C // P
 AHEAD = 2
+SG_AHEAD = 2
+GAIN_AFTER = 2
 EPS = 1e-6
 
 FLOPS = 2 * POINTS * DIMS * KV * C
@@ -34,14 +37,14 @@ def tile_selfinteraction_pb_t_kernel(tc, s, v, g_v, wv, ln_g1, out):
     nc = tc.nc
     with ExitStack() as ctx:
         const = ctx.enter_context(tc.tile_pool(name="const", bufs=1))
-        sg_pool = ctx.enter_context(tc.tile_pool(name="sg_pool", bufs=3))
+        sg_pool = ctx.enter_context(tc.tile_pool(name="sg_pool", bufs=SG_AHEAD + 1))
         gate_pool = ctx.enter_context(tc.tile_pool(name="gate_pool", bufs=AHEAD + 1))
         mx_pool = ctx.enter_context(tc.tile_pool(name="mx_pool", bufs=2))
         y_pool = ctx.enter_context(tc.tile_pool(name="y_pool", bufs=5))
         o_pool = ctx.enter_context(tc.tile_pool(name="o_pool", bufs=GROUP + 5))
         stat_pool = ctx.enter_context(tc.tile_pool(name="stat_pool", bufs=3))
         flip_psum = ctx.enter_context(tc.psum_pool(name="flip_psum", bufs=AHEAD))
-        dv_psum = ctx.enter_context(tc.psum_pool(name="dv_psum", bufs=2 * C_BLOCKS))
+        dv_psum = ctx.enter_context(tc.psum_pool(name="dv_psum", bufs=2 * C_CHUNKS))
         ctx.enter_context(tc.manual_schedule())
 
         s_dram = s.rearrange("(p i) c -> p i c", i=TILES)
@@ -62,8 +65,9 @@ def tile_selfinteraction_pb_t_kernel(tc, s, v, g_v, wv, ln_g1, out):
             if g == 0:
                 nc.sync.dma_start(
                     out=wv_rows[:].rearrange("q (h e) c -> q h e c", e=PAIR),
-                    in_=wv.rearrange("(h q e) c -> q h e c", h=2, e=PAIR),
+                    in_=wv.rearrange("(h q e) c -> q h e c", h=PARTS, e=PAIR),
                 )
+            if g == GAIN_AFTER:
                 nc.sync.dma_start(out=gain_sb[:], in_=ln_g1.partition_broadcast(P))
 
         v_words = v_sb[:].bitcast(F32)
@@ -121,7 +125,7 @@ def tile_selfinteraction_pb_t_kernel(tc, s, v, g_v, wv, ln_g1, out):
             sg_t_of[i] = sg_t
 
         def fetch_gates(i):
-            gates = gate_pool.tile([P, 2, P, PAIR], F32, tag="gates")
+            gates = gate_pool.tile([P, PARTS, P, PAIR], F32, tag="gates")
             nc.scalar.copy(
                 out=gates[:, 0, :, :],
                 in_=vg_t_of[i][:, DIMS * P : (DIMS + 1) * P]
@@ -143,17 +147,19 @@ def tile_selfinteraction_pb_t_kernel(tc, s, v, g_v, wv, ln_g1, out):
                     [P, DIMS, GROUP, P, PACK], BF16, align_bytes=64, tag="u_grouped"
                 )
                 u_grouped_of[g] = u_grouped
-            halves = vg_t_of[i][:].bitcast(BF16)
+            vg_t_bf16 = vg_t_of[i][:].bitcast(BF16)
             for d in range(DIMS):
                 first = place(d)
                 apart = place(DIMS + d) - first
-                v_pair = halves[:, first : first + PAIR * apart].rearrange("q (e w) -> q e w", e=PAIR)
+                v_pair = vg_t_bf16[:, first : first + PAIR * apart].rearrange(
+                    "q (e w) -> q e w", e=PAIR
+                )
                 nc.vector.tensor_tensor(
                     out=u_grouped_of[g][:, d, k, :, :].rearrange("q n (h e) -> q n h e", e=PAIR),
                     in0=v_pair[:, :, 0 : PAIR * P : PAIR]
                     .rearrange("q e n -> q n e")
                     .unsqueeze(2)
-                    .to_broadcast([P, P, 2, PAIR]),
+                    .to_broadcast([P, P, PARTS, PAIR]),
                     in1=gates_of[i][:].rearrange("q h n e -> q n h e"),
                     op=MULT,
                 )
@@ -173,8 +179,8 @@ def tile_selfinteraction_pb_t_kernel(tc, s, v, g_v, wv, ln_g1, out):
         def project(i):
             g, k = divmod(i, GROUP)
             points = slice(k * P, (k + 1) * P)
-            for block in range(C_BLOCKS):
-                cols = slice(block * P, (block + 1) * P)
+            for chunk in range(C_CHUNKS):
+                cols = slice(chunk * P, (chunk + 1) * P)
                 dv = dv_psum.tile([P, DIMS, P], F32, tag="dv")
                 for d in range(DIMS):
                     nc.tensor.matmul_mx(
@@ -186,15 +192,15 @@ def tile_selfinteraction_pb_t_kernel(tc, s, v, g_v, wv, ln_g1, out):
                         start=True,
                         stop=True,
                     )
-                dv_of[(i, block)] = dv
+                dv_of[(i, chunk)] = dv
 
         def residual(i):
             y = y_pool.tile([P, C, DIMS], F32, tag="y")
-            for block in range(C_BLOCKS):
-                cols = slice(block * P, (block + 1) * P)
+            for chunk in range(C_CHUNKS):
+                cols = slice(chunk * P, (chunk + 1) * P)
                 nc.vector.scalar_tensor_tensor(
                     out=y[:, cols, :],
-                    in0=dv_of[(i, block)][:].rearrange("p d c -> p c d"),
+                    in0=dv_of[(i, chunk)][:].rearrange("p d c -> p c d"),
                     scalar=1.0 / math.sqrt(KV),
                     in1=v_cd[:, i, cols, :],
                     op0=MULT,
@@ -236,8 +242,8 @@ def tile_selfinteraction_pb_t_kernel(tc, s, v, g_v, wv, ln_g1, out):
             nc.scalar.activation(out=o[:], in_=o[:], func=ACT.Copy, scale=inv_rms_of[g][:, k : k + 1])
             nc.sync.dma_start(out=out_dram[:, i, :, :], in_=o[:])
 
-        scalar_gates(0)
-        scalar_gates(1)
+        for g in range(SG_AHEAD):
+            scalar_gates(g)
         for i in range(AHEAD):
             flip(i)
             fetch_gates(i)
@@ -271,8 +277,8 @@ def tile_selfinteraction_pb_t_kernel(tc, s, v, g_v, wv, ln_g1, out):
                 if tile_y % GROUP == GROUP - 1:
                     inverse_rms(tile_y // GROUP)
                 apply_gain(tile_y)
-            if starts_group and tile_u // GROUP + 2 < GROUPS:
-                scalar_gates(tile_u // GROUP + 2)
+            if starts_group and tile_u // GROUP + SG_AHEAD < GROUPS:
+                scalar_gates(tile_u // GROUP + SG_AHEAD)
             if tile_u + AHEAD < TILES:
                 fetch_gates(tile_u + AHEAD)
             if 0 <= tile_o < TILES:

import math
from contextlib import ExitStack

import concourse.mybir as mybir
from concourse.masks import make_identity

BF16 = mybir.dt.bfloat16
F32 = mybir.dt.float32
U32 = mybir.dt.uint32
U8 = mybir.dt.uint8
FP8X4 = mybir.dt.float8_e4m3fn_x4
MULT = mybir.AluOpType.mult
ADD = mybir.AluOpType.add
ACT = mybir.ActivationFunctionType

P = 128
POINTS = 4096
C = 256
DIMS = 3
KV = 2 * C
PACK = 4
PAIR = 2
PARTS = 2
TILES = POINTS // P
GROUP = 2
GROUPS = TILES // GROUP
C_CHUNKS = C // P
AHEAD = 2
SG_AHEAD = 2
GAIN_AFTER = 2
EPS = 1e-6

FLOPS = 2 * POINTS * DIMS * KV * C


def tile_selfinteraction_pb_t_kernel(tc, s, v, g_v, wv, ln_g1, out):
    nc = tc.nc
    with ExitStack() as ctx:
        const = ctx.enter_context(tc.tile_pool(name="const", bufs=1))
        sg_pool = ctx.enter_context(tc.tile_pool(name="sg_pool", bufs=SG_AHEAD + 1))
        gate_pool = ctx.enter_context(tc.tile_pool(name="gate_pool", bufs=AHEAD + 1))
        mx_pool = ctx.enter_context(tc.tile_pool(name="mx_pool", bufs=2))
        y_pool = ctx.enter_context(tc.tile_pool(name="y_pool", bufs=5))
        o_pool = ctx.enter_context(tc.tile_pool(name="o_pool", bufs=GROUP + 5))
        stat_pool = ctx.enter_context(tc.tile_pool(name="stat_pool", bufs=3))
        flip_psum = ctx.enter_context(tc.psum_pool(name="flip_psum", bufs=AHEAD))
        dv_psum = ctx.enter_context(tc.psum_pool(name="dv_psum", bufs=2 * C_CHUNKS))
        ctx.enter_context(tc.manual_schedule())

        s_dram = s.rearrange("(p i) c -> p i c", i=TILES)
        g_dram = g_v.rearrange("(p i) m -> p i m", i=TILES)
        v_dram = v.rearrange("(p i) c d -> p i (c d)", i=TILES)
        out_dram = out.rearrange("(p i) c d -> p i c d", i=TILES)

        s_sb = const.tile([P, TILES, C], BF16)
        g_sb = const.tile([P, TILES, KV], BF16)
        v_sb = const.tile([P, TILES, C * DIMS], BF16)
        wv_rows = const.tile([P, PACK, C], BF16)
        gain_sb = const.tile([P, C], BF16)
        for g in range(GROUPS):
            tiles = slice(g * GROUP, (g + 1) * GROUP)
            nc.sync.dma_start(out=s_sb[:, tiles, :], in_=s_dram[:, tiles, :])
            nc.sync.dma_start(out=g_sb[:, tiles, :], in_=g_dram[:, tiles, :])
            nc.sync.dma_start(out=v_sb[:, tiles, :], in_=v_dram[:, tiles, :])
            if g == 0:
                nc.sync.dma_start(
                    out=wv_rows[:].rearrange("q (h e) c -> q h e c", e=PAIR),
                    in_=wv.rearrange("(h q e) c -> q h e c", h=PARTS, e=PAIR),
                )
            if g == GAIN_AFTER:
                nc.sync.dma_start(out=gain_sb[:], in_=ln_g1.partition_broadcast(P))

        v_words = v_sb[:].bitcast(F32)
        g_words = g_sb[:].bitcast(F32)
        v_cd = v_sb[:].rearrange("p i (c d) -> p i c d", d=DIMS)

        ident = const.tile([P, P], F32)
        make_identity(nc, ident[:])
        eps_sb = const.tile([P, 1], F32)
        nc.vector.memset(eps_sb[:], EPS)
        table_warmer = const.tile([P, 1], F32)
        nc.scalar.activation(out=table_warmer[:], in_=eps_sb[:], func=ACT.Abs_reciprocal_sqrt)

        sg_of = {}
        vg_t_of = {}
        sg_t_of = {}
        gates_of = {}
        u_grouped_of = {}
        u_codes_of = {}
        u_scales_of = {}
        dv_of = {}
        y_of = {}
        o_of = {}
        sum_sq_of = {}
        inv_rms_of = {}

        def scalar_gates(g):
            tiles = slice(g * GROUP, (g + 1) * GROUP)
            sg = sg_pool.tile([P, GROUP, PAIR, P], F32, tag="sg")
            nc.gpsimd.tensor_tensor(
                out=sg[:],
                in0=s_sb[:, tiles, :].rearrange("p k (q e) -> p k e q", e=PAIR),
                in1=g_sb[:, tiles, C:KV].rearrange("p k (q e) -> p k e q", e=PAIR),
                op=MULT,
            )
            sg_of[g] = sg

        def flip(i):
            vg_t = flip_psum.tile([P, (DIMS + 1) * P], F32, tag="vg_t")
            for r in range(DIMS):
                nc.tensor.transpose(
                    out=vg_t[:, r * P : (r + 1) * P],
                    in_=v_words[:, i, r : DIMS * P : DIMS],
                    identity=ident[:],
                )
            nc.tensor.transpose(
                out=vg_t[:, DIMS * P : (DIMS + 1) * P], in_=g_words[:, i, 0:P], identity=ident[:]
            )
            sg_t = flip_psum.tile([P, PAIR, P], F32, tag="sg_t")
            for e in range(PAIR):
                nc.tensor.transpose(
                    out=sg_t[:, e, :], in_=sg_of[i // GROUP][:, i % GROUP, e, :], identity=ident[:]
                )
            vg_t_of[i] = vg_t
            sg_t_of[i] = sg_t

        def fetch_gates(i):
            gates = gate_pool.tile([P, PARTS, P, PAIR], F32, tag="gates")
            nc.scalar.copy(
                out=gates[:, 0, :, :],
                in_=vg_t_of[i][:, DIMS * P : (DIMS + 1) * P]
                .bitcast(BF16)
                .rearrange("q (n e) -> q n e", e=PAIR),
            )
            nc.scalar.mul(
                out=gates[:, 1, :, :], in_=sg_t_of[i][:].rearrange("q e n -> q n e"), mul=math.sqrt(2.0)
            )
            gates_of[i] = gates

        def place(f):
            return PAIR * P * (f // PAIR) + f % PAIR

        def gate_product(i):
            g, k = divmod(i, GROUP)
            if k == 0:
                u_grouped = mx_pool.tile(
                    [P, DIMS, GROUP, P, PACK], BF16, align_bytes=64, tag="u_grouped"
                )
                u_grouped_of[g] = u_grouped
            vg_t_bf16 = vg_t_of[i][:].bitcast(BF16)
            for d in range(DIMS):
                first = place(d)
                apart = place(DIMS + d) - first
                v_pair = vg_t_bf16[:, first : first + PAIR * apart].rearrange(
                    "q (e w) -> q e w", e=PAIR
                )
                nc.vector.tensor_tensor(
                    out=u_grouped_of[g][:, d, k, :, :].rearrange("q n (h e) -> q n h e", e=PAIR),
                    in0=v_pair[:, :, 0 : PAIR * P : PAIR]
                    .rearrange("q e n -> q n e")
                    .unsqueeze(2)
                    .to_broadcast([P, P, PARTS, PAIR]),
                    in1=gates_of[i][:].rearrange("q h n e -> q n h e"),
                    op=MULT,
                )

        def quantise(g):
            u_codes = mx_pool.tile([P, DIMS, GROUP * P], U32, align_bytes=64, tag="u_codes")
            u_scales = mx_pool.tile([P, DIMS, GROUP * P], U8, align_bytes=64, tag="u_scales")
            for d in range(DIMS):
                nc.vector.quantize_mx(
                    out=u_codes[:, d, :].bitcast(FP8X4),
                    scales=u_scales[:, d, :],
                    in_=u_grouped_of[g][:, d, :, :, :].rearrange("q k n t -> q (k n t)"),
                )
            u_codes_of[g] = u_codes
            u_scales_of[g] = u_scales

        def project(i):
            g, k = divmod(i, GROUP)
            points = slice(k * P, (k + 1) * P)
            for chunk in range(C_CHUNKS):
                cols = slice(chunk * P, (chunk + 1) * P)
                dv = dv_psum.tile([P, DIMS, P], F32, tag="dv")
                for d in range(DIMS):
                    nc.tensor.matmul_mx(
                        out=dv[:, d, :],
                        lhsT=u_codes_of[g][:, d, points].bitcast(FP8X4),
                        lhsT_scale=u_scales_of[g][:, d, points],
                        rhs=wv_codes[:, cols].bitcast(FP8X4),
                        rhs_scale=wv_scales[:, cols],
                        start=True,
                        stop=True,
                    )
                dv_of[(i, chunk)] = dv

        def residual(i):
            y = y_pool.tile([P, C, DIMS], F32, tag="y")
            for chunk in range(C_CHUNKS):
                cols = slice(chunk * P, (chunk + 1) * P)
                nc.vector.scalar_tensor_tensor(
                    out=y[:, cols, :],
                    in0=dv_of[(i, chunk)][:].rearrange("p d c -> p c d"),
                    scalar=1.0 / math.sqrt(KV),
                    in1=v_cd[:, i, cols, :],
                    op0=MULT,
                    op1=ADD,
                )
            y_of[i] = y

        def sum_squares(i):
            g, k = divmod(i, GROUP)
            if k == 0:
                sum_sq = stat_pool.tile([P, GROUP], F32, tag="sum_sq")
                sum_sq_of[g] = sum_sq
            squares = y_pool.tile([P, C, DIMS], BF16, tag="squares")
            nc.scalar.activation(
                out=squares[:], in_=y_of[i][:], func=ACT.Square, accum_out=sum_sq_of[g][:, k : k + 1]
            )

        def inverse_rms(g):
            inv_rms = stat_pool.tile([P, GROUP], F32, tag="inv_rms")
            nc.scalar.activation(
                out=inv_rms[:],
                in_=sum_sq_of[g][:],
                func=ACT.Abs_reciprocal_sqrt,
                bias=eps_sb[:],
                scale=1.0 / (C * DIMS),
            )
            inv_rms_of[g] = inv_rms

        def apply_gain(i):
            o = o_pool.tile([P, C, DIMS], F32, tag="o")
            nc.gpsimd.tensor_tensor(
                out=o[:], in0=y_of[i][:], in1=gain_sb[:].unsqueeze(2).to_broadcast([P, C, DIMS]), op=MULT
            )
            o_of[i] = o

        def normalise_and_store(i):
            g, k = divmod(i, GROUP)
            o = o_of[i]
            nc.scalar.activation(out=o[:], in_=o[:], func=ACT.Copy, scale=inv_rms_of[g][:, k : k + 1])
            nc.sync.dma_start(out=out_dram[:, i, :, :], in_=o[:])

        for g in range(SG_AHEAD):
            scalar_gates(g)
        for i in range(AHEAD):
            flip(i)
            fetch_gates(i)

        wv_grouped = const.tile([P, C, PACK], BF16, align_bytes=64)
        nc.vector.tensor_copy(out=wv_grouped[:], in_=wv_rows[:].rearrange("q t c -> q c t"))
        wv_codes = const.tile([P, C], U32, align_bytes=64)
        wv_scales = const.tile([P, C], U8, align_bytes=64)
        nc.vector.quantize_mx(
            out=wv_codes[:].bitcast(FP8X4),
            scales=wv_scales[:],
            in_=wv_grouped[:].rearrange("q c t -> q (c t)"),
        )

        for tile_u in range(TILES + 2 * GROUP + 1):
            tile_y = tile_u - GROUP - 1
            tile_o = tile_y - GROUP
            starts_group = tile_u % GROUP == 0
            if 0 <= tile_y < TILES:
                project(tile_y)
            if tile_u < TILES:
                gate_product(tile_u)
            if tile_u + AHEAD < TILES:
                flip(tile_u + AHEAD)
            if 0 <= tile_y < TILES:
                residual(tile_y)
            if starts_group and 1 <= tile_u // GROUP <= GROUPS:
                quantise(tile_u // GROUP - 1)
            if 0 <= tile_y < TILES:
                sum_squares(tile_y)
                if tile_y % GROUP == GROUP - 1:
                    inverse_rms(tile_y // GROUP)
                apply_gain(tile_y)
            if starts_group and tile_u // GROUP + SG_AHEAD < GROUPS:
                scalar_gates(tile_u // GROUP + SG_AHEAD)
            if tile_u + AHEAD < TILES:
                fetch_gates(tile_u + AHEAD)
            if 0 <= tile_o < TILES:
                normalise_and_store(tile_o)
